import numpy as np
import ml_dtypes


def mxq(x, axis, fmt="e4m3"):
    dtype, down = {"e4m3": (ml_dtypes.float8_e4m3fn, 7), "e5m2": (ml_dtypes.float8_e5m2, 14)}[fmt]
    v = np.moveaxis(np.asarray(x, np.float32).astype(ml_dtypes.bfloat16).astype(np.float64), axis, -1)
    blocks = v.reshape(v.shape[:-1] + (-1, 32))
    amax = np.abs(blocks).max(-1, keepdims=True)
    byte = np.maximum(np.where(amax > 0, np.frexp(amax)[1] - 1 + 127, 0) - down, 1)
    scale = np.exp2(byte - 127.0)
    codes = (blocks / scale).astype(np.float32).astype(dtype).astype(np.float64)
    return np.moveaxis((codes * scale).reshape(v.shape), -1, axis)


WIDE = False


def mx_kscale(k):
    if not WIDE:
        return np.ones(k)
    levels = np.array([10, -10, 5, -5, 0])
    a = np.random.permutation(np.resize(levels, k // 512 * 4)).reshape(k // 512, 4)
    idx = np.arange(k)
    return np.exp2(a[idx // 512, idx % 128 // 32])


BF16 = ml_dtypes.bfloat16


def bf(x):
    return np.asarray(x, np.float32).astype(BF16)


def f64(x):
    return np.asarray(x).astype(np.float64)


B, F0, FK, S1, S2, D = 64, 64, 128, 128, 128, 16
M1 = F0 * FK
M2 = F0 * S1


def setup_inputs():
    u = mx_kscale(M2).reshape(F0, S1)[:, 0]
    t = mx_kscale(M1).reshape(F0, FK)[0]
    w1 = np.random.standard_normal((F0, FK, S1)) / np.sqrt(M1) / u[:, None, None] / t[None, :, None]
    w2 = np.random.standard_normal((F0, S1, S2)) / np.sqrt(M2) / u[:, None, None]
    return {"x": bf(np.random.standard_normal((B, F0, D)) * u[None, :, None]),
            "x1": bf(np.random.standard_normal((B, FK, D)) * t[None, :, None]),
            "w1": bf(w1.reshape(M1, S1)), "b1": bf(np.random.standard_normal(S1) * 0.2),
            "w2": bf(w2.reshape(M2, S2)), "b2": bf(np.random.standard_normal(S2) * 0.2)}


def reference(x, x1, w1, b1, w2, b2):
    x0 = f64(x).transpose(0, 2, 1)
    xk = f64(x1).transpose(0, 2, 1)
    z1 = (x0[:, :, :, None] * xk[:, :, None, :]).reshape(B, D, M1)
    o1 = (mxq(z1, 2, "e4m3") @ mxq(f64(w1), 0, "e4m3")) + f64(b1)
    z2 = (x0[:, :, :, None] * o1[:, :, None, :]).reshape(B, D, M2)
    o2 = (mxq(z2, 2, "e4m3") @ mxq(f64(w2), 0, "e4m3")) + f64(b2)
    return np.concatenate([o1.sum(axis=1), o2.sum(axis=1)], axis=1)

@@ -1,0 +1,221 @@
+from contextlib import ExitStack
+
+import concourse.mybir as mybir
+from concourse.masks import make_identity
+
+F32 = mybir.dt.float32
+BF16 = mybir.dt.bfloat16
+U32 = mybir.dt.uint32
+U8 = mybir.dt.uint8
+FP8X4 = mybir.dt.float8_e4m3fn_x4
+MULT = mybir.AluOpType.mult
+ADD = mybir.AluOpType.add
+
+P = 128
+B, F0, FK, S, D = 64, 64, 128, 128, 16
+N = B * D
+K = F0 * FK
+K_PASS = 4 * P
+PASSES = K // K_PASS
+N_TILES = N // P
+B_TILE = P // D
+CHUNK = 4
+CHUNKS = PASSES // CHUNK
+I_PASS = K_PASS // FK
+I_CHUNK = CHUNK * I_PASS
+LAYERS = 2
+
+FLOPS = LAYERS * 2 * N * K * S
+
+
+def tile_cin_pa_kernel(tc, x, x1, w1, b1, w2, b2, out):
+    nc = tc.nc
+    weights = (w1, w2)
+    with ExitStack() as stack:
+        keep = stack.enter_context(tc.tile_pool(name="keep", bufs=1))
+        stage = stack.enter_context(tc.tile_pool(name="stage", bufs=3))
+
+        x_fields = keep.tile([P, N // 2], BF16)
+        for h in range(2):
+            nc.sync.dma_start(
+                out=x_fields[F0 * h : F0 * (h + 1), :].rearrange("i (b d) -> i b d", d=D),
+                in_=x[B // 2 * h : B // 2 * (h + 1)].rearrange("b i d -> i b d"),
+            )
+        x1_fields = keep.tile([P, N], BF16)
+        for quarter in range(4):
+            nc.sync.dma_start(
+                out=x1_fields[:, N // 4 * quarter : N // 4 * (quarter + 1)].rearrange("j (b d) -> j b d", d=D),
+                in_=x1[B // 4 * quarter : B // 4 * (quarter + 1)].rearrange("b j d -> j b d"),
+            )
+        bias_bf = keep.tile([P, LAYERS, S], BF16)
+        nc.sync.dma_start(out=bias_bf[:, 0, :], in_=b1.partition_broadcast(P))
+        nc.sync.dma_start(out=bias_bf[:, 1, :], in_=b2.partition_broadcast(P))
+        w_rows = []
+        for layer in range(LAYERS):
+            rows = keep.tile([P, PASSES, 4, S], BF16, name="w_rows%d" % layer)
+            w_rows.append(rows)
+            source = weights[layer].rearrange("(c u p e) s -> p c u (e s)", c=CHUNKS, p=P, e=2)
+            for c in range(CHUNKS):
+                nc.scalar.dma_start(
+                    out=rows[:, CHUNK * c : CHUNK * (c + 1), :, :].rearrange("p g (u e) s -> p (g u) (e s)", e=2),
+                    in_=source[:, c, :, :],
+                )
+
+        ident_bf = keep.tile([P, P], BF16)
+        make_identity(nc, ident_bf[:])
+        ident_f = keep.tile([P, P], F32)
+        make_identity(nc, ident_f[:])
+        pool_first = B - B_TILE
+        pool_sel = keep.tile([P, pool_first + P], F32)
+        nc.vector.memset(pool_sel[:], 0.0)
+        nc.vector.tensor_reduce(
+            out=pool_sel[:, pool_first : pool_first + B_TILE],
+            in_=ident_f[:].rearrange("p (b d) -> p b d", d=D),
+            axis=mybir.AxisListType.X,
+            op=ADD,
+        )
+        bias_f = keep.tile([P, LAYERS, S], F32)
+        nc.vector.tensor_copy(out=bias_f[:], in_=bias_bf[:])
+
+        x_scalar = keep.tile([P, 4, 2, F0], F32)
+        x_pairs = keep.tile([P, 4, 2, F0, 2], BF16)
+        x1_rows = keep.tile([P, N_TILES, FK], BF16)
+        with tc.psum_pool(name="head", bufs=1) as head:
+            x_t = head.tile([P, 4, P], BF16)
+            for m in range(4):
+                nc.tensor.transpose(x_t[:, m, :], x_fields[:, P * m : P * (m + 1)], ident_bf[:])
+            x1_t = head.tile([P, N_TILES, P], BF16)
+            for t in range(N_TILES):
+                nc.tensor.transpose(x1_t[:, t, :], x1_fields[:, P * t : P * (t + 1)], ident_bf[:])
+            x_flat = x_t[:].rearrange("p m c -> p (m c)")
+            nc.vector.tensor_copy(out=x_scalar[:].rearrange("p m h i -> p (m h i)"), in_=x_flat)
+            nc.scalar.copy(
+                out=x_pairs[:].rearrange("p m h i r -> p (m h i) r"),
+                in_=x_flat.unsqueeze(2).to_broadcast([P, 4 * P, 2]),
+            )
+            nc.vector.tensor_copy(out=x1_rows[:], in_=x1_t[:])
+
+        turn = stack.enter_context(tc.psum_pool(name="turn", bufs=4))
+        sums = stack.enter_context(tc.psum_pool(name="sums", bufs=2))
+        total = stack.enter_context(tc.psum_pool(name="total", bufs=1))
+
+        w_codes = [keep.tile([P, PASSES, S], U32, name="w_codes%d" % l, align_bytes=64) for l in range(LAYERS)]
+        w_scales = [keep.tile([P, PASSES, S], U8, name="w_scales%d" % l, align_bytes=64) for l in range(LAYERS)]
+        pooled = total.tile([P, LAYERS * S], F32)
+
+        def prepare_weights(layer, first, count):
+            w_grouped = stage.tile([P, count, S, 4], BF16, align_bytes=64, tag="w_grouped%d" % count)
+            nc.scalar.copy(
+                out=w_grouped[:],
+                in_=w_rows[layer][:, first : first + count, :, :].rearrange("p g t s -> p g s t"),
+            )
+            nc.vector.quantize_mx(
+                out=w_codes[layer][:, first : first + count, :].rearrange("p g s -> p (g s)").bitcast(FP8X4),
+                scales=w_scales[layer][:, first : first + count, :].rearrange("p g s -> p (g s)"),
+                in_=w_grouped[:].rearrange("p g s t -> p (g s t)"),
+            )
+
+        units = [(0, 0)]
+        for t in range(1, N_TILES):
+            units.extend([(0, t), (1, t - 1)])
+        units.append((1, N_TILES - 1))
+        chunks = [(layer, t, c) for (layer, t) in units for c in range(CHUNKS)]
+
+        z_rows, z_grouped, z_codes, z_scales, acc, o12 = {}, {}, {}, {}, {}, {}
+
+        def form_products(step):
+            layer, t, c = chunks[step]
+            m, h = t % 4, t // 4
+            first_i = I_CHUNK * c
+            z = stage.tile([P, I_CHUNK * FK], BF16, name="z_rows")
+            z_rows[step] = z
+            if layer == 0:
+                shape = [P, I_CHUNK, FK // 2, 2]
+                nc.vector.tensor_tensor(
+                    out=z[:].rearrange("p (i j r) -> p i j r", i=I_CHUNK, r=2),
+                    in0=x1_rows[:, t, :].rearrange("p (j r) -> p j r", r=2).unsqueeze(1).to_broadcast(shape),
+                    in1=x_pairs[:, m, h, first_i : first_i + I_CHUNK, :].unsqueeze(2).to_broadcast(shape),
+                    op=MULT,
+                )
+            else:
+                for i in range(I_CHUNK):
+                    nc.vector.tensor_scalar(
+                        out=z[:, FK * i : FK * (i + 1)],
+                        in0=o12[t][:, 0:S],
+                        scalar1=x_scalar[:, m, h, first_i + i : first_i + i + 1],
+                        scalar2=None,
+                        op0=MULT,
+                    )
+
+        def turn_to_k(step):
+            words = z_rows[step][:].bitcast(F32)
+            grouped = stage.tile([P, CHUNK * P * 4], BF16, name="z_grouped", align_bytes=64)
+            z_grouped[step] = grouped
+            grouped_words = grouped[:].bitcast(F32).rearrange("p (a n u) -> p a n u", a=CHUNK, u=2)
+            for half in range(CHUNK // 2):
+                bank = turn.tile([P, 2, 2, P], F32, name="bank")
+                for a in range(2):
+                    for u in range(2):
+                        first = P * (4 * half + 2 * a + u)
+                        nc.tensor.transpose(bank[:, a, u, :], words[:, first : first + P], ident_f[:])
+                nc.scalar.copy(
+                    out=grouped_words[:, 2 * half : 2 * half + 2, :, :],
+                    in_=bank[:].rearrange("p a u n -> p a n u"),
+                )
+
+        def quantise(step):
+            codes = stage.tile([P, CHUNK * P], U32, name="z_codes", align_bytes=64)
+            scales = stage.tile([P, CHUNK * P], U8, name="z_scales", align_bytes=64)
+            z_codes[step], z_scales[step] = codes, scales
+            nc.vector.quantize_mx(out=codes[:].bitcast(FP8X4), scales=scales[:], in_=z_grouped[step][:])
+
+        def multiply(step):
+            layer, t, c = chunks[step]
+            if c == 0:
+                acc[(layer, t)] = sums.tile([P, S], F32, name="acc")
+            group = acc[(layer, t)]
+            for a in range(CHUNK):
+                g = CHUNK * c + a
+                nc.tensor.matmul_mx(
+                    out=group[:],
+                    lhsT=z_codes[step][:, P * a : P * (a + 1)].bitcast(FP8X4),
+                    lhsT_scale=z_scales[step][:, P * a : P * (a + 1)],
+                    rhs=w_codes[layer][:, g, :].bitcast(FP8X4),
+                    rhs_scale=w_scales[layer][:, g, :],
+                    start=(g == 0),
+                    stop=(g == PASSES - 1),
+                )
+            if c < CHUNKS - 1:
+                return
+            if layer == 0:
+                o12[t] = stage.tile([P, LAYERS * S], F32, name="o12")
+            nc.vector.tensor_tensor(
+                out=o12[t][:, S * layer : S * (layer + 1)], in0=group[:], in1=bias_f[:, layer, :], op=ADD
+            )
+            if layer == 1:
+                window = pool_first - B_TILE * t
+                nc.tensor.matmul(
+                    out=pooled[:],
+                    lhsT=pool_sel[:, window : window + P],
+                    rhs=o12[t][:],
+                    start=(t == 0),
+                    stop=(t == N_TILES - 1),
+                )
+
+        for step in range(len(chunks) + 3):
+            if step < len(chunks):
+                form_products(step)
+            if step < CHUNKS:
+                prepare_weights(0, CHUNK * step, CHUNK)
+            elif step < 3 * CHUNKS:
+                prepare_weights(1, 2 * (step - CHUNKS), 2)
+            if 0 <= step - 1 < len(chunks):
+                turn_to_k(step - 1)
+            if 0 <= step - 2 < len(chunks):
+                quantise(step - 2)
+            if 0 <= step - 3 < len(chunks):
+                multiply(step - 3)
+
+        result = keep.tile([P, LAYERS * S], F32)
+        nc.vector.tensor_copy(out=result[:], in_=pooled[:])
+        nc.sync.dma_start(out=out[:, :], in_=result[0:B, :])

@@ -19,7 +19,9 @@ K_PASS = 4 * P
 PASSES = K // K_PASS
 N_TILES = N // P
 B_TILE = P // D
-CHUNK = 4
+CHUNK = 8
+LOAD = 4
+LEAD = 2
 CHUNKS = PASSES // CHUNK
 I_PASS = K_PASS // FK
 I_CHUNK = CHUNK * I_PASS
@@ -54,10 +56,10 @@ def tile_cin_pa_kernel(tc, x, x1, w1, b1, w2, b2, out):
         for layer in range(LAYERS):
             rows = keep.tile([P, PASSES, 4, S], BF16, name="w_rows%d" % layer)
             w_rows.append(rows)
-            source = weights[layer].rearrange("(c u p e) s -> p c u (e s)", c=CHUNKS, p=P, e=2)
-            for c in range(CHUNKS):
+            source = weights[layer].rearrange("(c u p e) s -> p c u (e s)", c=PASSES // LOAD, p=P, e=2)
+            for c in range(PASSES // LOAD):
                 nc.scalar.dma_start(
-                    out=rows[:, CHUNK * c : CHUNK * (c + 1), :, :].rearrange("p g (u e) s -> p (g u) (e s)", e=2),
+                    out=rows[:, LOAD * c : LOAD * (c + 1), :, :].rearrange("p g (u e) s -> p (g u) (e s)", e=2),
                     in_=source[:, c, :, :],
                 )
 
@@ -76,6 +78,24 @@ def tile_cin_pa_kernel(tc, x, x1, w1, b1, w2, b2, out):
         )
         bias_f = keep.tile([P, LAYERS, S], F32)
         nc.vector.tensor_copy(out=bias_f[:], in_=bias_bf[:])
+
+        w_codes = [keep.tile([P, PASSES, S], U32, name="w_codes%d" % l, align_bytes=64) for l in range(LAYERS)]
+        w_scales = [keep.tile([P, PASSES, S], U8, name="w_scales%d" % l, align_bytes=64) for l in range(LAYERS)]
+
+        def prepare_weights(layer, first, count, copy):
+            w_grouped = stage.tile([P, count, S, 4], BF16, align_bytes=64, tag="w_grouped%d" % count)
+            copy(
+                out=w_grouped[:],
+                in_=w_rows[layer][:, first : first + count, :, :].rearrange("p g t s -> p g s t"),
+            )
+            nc.vector.quantize_mx(
+                out=w_codes[layer][:, first : first + count, :].rearrange("p g s -> p (g s)").bitcast(FP8X4),
+                scales=w_scales[layer][:, first : first + count, :].rearrange("p g s -> p (g s)"),
+                in_=w_grouped[:].rearrange("p g s t -> p (g s t)"),
+            )
+
+        for c in range(PASSES // LOAD):
+            prepare_weights(0, LOAD * c, LOAD, nc.scalar.copy if c % 2 == 0 else nc.vector.tensor_copy)
 
         x_scalar = keep.tile([P, 4, 2, F0], F32)
         x_pairs = keep.tile([P, 4, 2, F0, 2], BF16)
@@ -99,26 +119,14 @@ def tile_cin_pa_kernel(tc, x, x1, w1, b1, w2, b2, out):
         sums = stack.enter_context(tc.psum_pool(name="sums", bufs=2))
         total = stack.enter_context(tc.psum_pool(name="total", bufs=1))
 
-        w_codes = [keep.tile([P, PASSES, S], U32, name="w_codes%d" % l, align_bytes=64) for l in range(LAYERS)]
-        w_scales = [keep.tile([P, PASSES, S], U8, name="w_scales%d" % l, align_bytes=64) for l in range(LAYERS)]
         pooled = total.tile([P, LAYERS * S], F32)
 
-        def prepare_weights(layer, first, count):
-            w_grouped = stage.tile([P, count, S, 4], BF16, align_bytes=64, tag="w_grouped%d" % count)
-            nc.scalar.copy(
-                out=w_grouped[:],
-                in_=w_rows[layer][:, first : first + count, :, :].rearrange("p g t s -> p g s t"),
-            )
-            nc.vector.quantize_mx(
-                out=w_codes[layer][:, first : first + count, :].rearrange("p g s -> p (g s)").bitcast(FP8X4),
-                scales=w_scales[layer][:, first : first + count, :].rearrange("p g s -> p (g s)"),
-                in_=w_grouped[:].rearrange("p g s t -> p (g s t)"),
-            )
-
-        units = [(0, 0)]
-        for t in range(1, N_TILES):
-            units.extend([(0, t), (1, t - 1)])
-        units.append((1, N_TILES - 1))
+        units = []
+        for t in range(N_TILES + LEAD):
+            if t < N_TILES:
+                units.append((0, t))
+            if t >= LEAD:
+                units.append((1, t - LEAD))
         chunks = [(layer, t, c) for (layer, t) in units for c in range(CHUNKS)]
 
         z_rows, z_grouped, z_codes, z_scales, acc, o12 = {}, {}, {}, {}, {}, {}
@@ -188,7 +196,7 @@ def tile_cin_pa_kernel(tc, x, x1, w1, b1, w2, b2, out):
             if c < CHUNKS - 1:
                 return
             if layer == 0:
-                o12[t] = stage.tile([P, LAYERS * S], F32, name="o12")
+                o12[t] = stage.tile([P, LAYERS * S], F32, name="o12", bufs=LEAD + 2)
             nc.vector.tensor_tensor(
                 out=o12[t][:, S * layer : S * (layer + 1)], in0=group[:], in1=bias_f[:, layer, :], op=ADD
             )
@@ -203,18 +211,16 @@ def tile_cin_pa_kernel(tc, x, x1, w1, b1, w2, b2, out):
                 )
 
         for step in range(len(chunks) + 3):
-            if step < len(chunks):
-                form_products(step)
-            if step < CHUNKS:
-                prepare_weights(0, CHUNK * step, CHUNK)
-            elif step < 3 * CHUNKS:
-                prepare_weights(1, 2 * (step - CHUNKS), 2)
-            if 0 <= step - 1 < len(chunks):
-                turn_to_k(step - 1)
-            if 0 <= step - 2 < len(chunks):
-                quantise(step - 2)
             if 0 <= step - 3 < len(chunks):
                 multiply(step - 3)
+            if 0 <= step - 2 < len(chunks):
+                quantise(step - 2)
+            if 0 <= step - 1 < len(chunks):
+                turn_to_k(step - 1)
+            if step < len(chunks):
+                form_products(step)
+            if 2 * step < PASSES:
+                prepare_weights(1, 2 * step, 2, nc.scalar.copy)
 
         result = keep.tile([P, LAYERS * S], F32)
         nc.vector.tensor_copy(out=result[:], in_=pooled[:])

@@ -10,6 +10,7 @@ U8 = mybir.dt.uint8
 FP8X4 = mybir.dt.float8_e4m3fn_x4
 MULT = mybir.AluOpType.mult
 ADD = mybir.AluOpType.add
+COPY = mybir.ActivationFunctionType.Copy
 
 P = 128
 B, F0, FK, S, D = 64, 64, 128, 128, 16
@@ -19,13 +20,12 @@ K_PASS = 4 * P
 PASSES = K // K_PASS
 N_TILES = N // P
 B_TILE = P // D
-CHUNK = 8
-LOAD = 4
-LEAD = 2
+CHUNK = 4
 CHUNKS = PASSES // CHUNK
 I_PASS = K_PASS // FK
 I_CHUNK = CHUNK * I_PASS
 LAYERS = 2
+SCALAR_EVERY = 4
 
 FLOPS = LAYERS * 2 * N * K * S
 
@@ -44,24 +44,34 @@ def tile_cin_pa_kernel(tc, x, x1, w1, b1, w2, b2, out):
                 in_=x[B // 2 * h : B // 2 * (h + 1)].rearrange("b i d -> i b d"),
             )
         x1_fields = keep.tile([P, N], BF16)
-        for quarter in range(4):
+
+        def load_x1(quarter):
             nc.sync.dma_start(
                 out=x1_fields[:, N // 4 * quarter : N // 4 * (quarter + 1)].rearrange("j (b d) -> j b d", d=D),
                 in_=x1[B // 4 * quarter : B // 4 * (quarter + 1)].rearrange("b j d -> j b d"),
             )
+
+        w_rows = [keep.tile([P, PASSES, 4, S], BF16, name="w_rows%d" % l) for l in range(LAYERS)]
+
+        def load_weights(layer):
+            source = weights[layer].rearrange("(c u p e) s -> p c u (e s)", c=CHUNKS, p=P, e=2)
+            for c in range(CHUNKS):
+                nc.sync.dma_start(
+                    out=w_rows[layer][:, CHUNK * c : CHUNK * (c + 1), :, :].rearrange(
+                        "p g (u e) s -> p (g u) (e s)", e=2
+                    ),
+                    in_=source[:, c, :, :],
+                )
+
+        load_x1(0)
         bias_bf = keep.tile([P, LAYERS, S], BF16)
         nc.sync.dma_start(out=bias_bf[:, 0, :], in_=b1.partition_broadcast(P))
         nc.sync.dma_start(out=bias_bf[:, 1, :], in_=b2.partition_broadcast(P))
-        w_rows = []
-        for layer in range(LAYERS):
-            rows = keep.tile([P, PASSES, 4, S], BF16, name="w_rows%d" % layer)
-            w_rows.append(rows)
-            source = weights[layer].rearrange("(c u p e) s -> p c u (e s)", c=PASSES // LOAD, p=P, e=2)
-            for c in range(PASSES // LOAD):
-                nc.scalar.dma_start(
-                    out=rows[:, LOAD * c : LOAD * (c + 1), :, :].rearrange("p g (u e) s -> p (g u) (e s)", e=2),
-                    in_=source[:, c, :, :],
-                )
+        load_weights(0)
+        load_x1(1)
+        load_weights(1)
+        load_x1(2)
+        load_x1(3)
 
         ident_bf = keep.tile([P, P], BF16)
         make_identity(nc, ident_bf[:])
@@ -79,8 +89,36 @@ def tile_cin_pa_kernel(tc, x, x1, w1, b1, w2, b2, out):
         bias_f = keep.tile([P, LAYERS, S], F32)
         nc.vector.tensor_copy(out=bias_f[:], in_=bias_bf[:])
 
+        x_scalar = keep.tile([P, 4, 2, F0], F32)
+        x_pairs = keep.tile([P, 4, 2, F0, 2], BF16)
+        x1_rows = keep.tile([P, N_TILES, FK], BF16)
+        head = stack.enter_context(tc.psum_pool(name="head", bufs=1))
+        x_t = head.tile([P, 4, P], BF16, tag="turned")
+        for m in range(4):
+            nc.tensor.transpose(x_t[:, m, :], x_fields[:, P * m : P * (m + 1)], ident_bf[:])
+        x_flat = x_t[:].rearrange("p m c -> p (m c)")
+        nc.vector.tensor_copy(out=x_scalar[:].rearrange("p m h i -> p (m h i)"), in_=x_flat)
+        nc.scalar.copy(
+            out=x_pairs[:].rearrange("p m h i r -> p (m h i) r"),
+            in_=x_flat.unsqueeze(2).to_broadcast([P, 4 * P, 2]),
+        )
+
+        def turn_x1(quarter):
+            x1_t = head.tile([P, 2, P], BF16, tag="turned")
+            for r in range(2):
+                t = 2 * quarter + r
+                nc.tensor.transpose(x1_t[:, r, :], x1_fields[:, P * t : P * (t + 1)], ident_bf[:])
+            nc.scalar.copy(out=x1_rows[:, 2 * quarter : 2 * quarter + 2, :], in_=x1_t[:])
+
+        turn_x1(0)
+
+        turn = stack.enter_context(tc.psum_pool(name="turn", bufs=4))
+        sums = stack.enter_context(tc.psum_pool(name="sums", bufs=2))
+        total = stack.enter_context(tc.psum_pool(name="total", bufs=1))
+
         w_codes = [keep.tile([P, PASSES, S], U32, name="w_codes%d" % l, align_bytes=64) for l in range(LAYERS)]
         w_scales = [keep.tile([P, PASSES, S], U8, name="w_scales%d" % l, align_bytes=64) for l in range(LAYERS)]
+        pooled = total.tile([P, LAYERS * S], F32)
 
         def prepare_weights(layer, first, count, copy):
             w_grouped = stage.tile([P, count, S, 4], BF16, align_bytes=64, tag="w_grouped%d" % count)
@@ -94,39 +132,10 @@ def tile_cin_pa_kernel(tc, x, x1, w1, b1, w2, b2, out):
                 in_=w_grouped[:].rearrange("p g s t -> p (g s t)"),
             )
 
-        for c in range(PASSES // LOAD):
-            prepare_weights(0, LOAD * c, LOAD, nc.scalar.copy if c % 2 == 0 else nc.vector.tensor_copy)
-
-        x_scalar = keep.tile([P, 4, 2, F0], F32)
-        x_pairs = keep.tile([P, 4, 2, F0, 2], BF16)
-        x1_rows = keep.tile([P, N_TILES, FK], BF16)
-        with tc.psum_pool(name="head", bufs=1) as head:
-            x_t = head.tile([P, 4, P], BF16)
-            for m in range(4):
-                nc.tensor.transpose(x_t[:, m, :], x_fields[:, P * m : P * (m + 1)], ident_bf[:])
-            x1_t = head.tile([P, N_TILES, P], BF16)
-            for t in range(N_TILES):
-                nc.tensor.transpose(x1_t[:, t, :], x1_fields[:, P * t : P * (t + 1)], ident_bf[:])
-            x_flat = x_t[:].rearrange("p m c -> p (m c)")
-            nc.vector.tensor_copy(out=x_scalar[:].rearrange("p m h i -> p (m h i)"), in_=x_flat)
-            nc.scalar.copy(
-                out=x_pairs[:].rearrange("p m h i r -> p (m h i) r"),
-                in_=x_flat.unsqueeze(2).to_broadcast([P, 4 * P, 2]),
-            )
-            nc.vector.tensor_copy(out=x1_rows[:], in_=x1_t[:])
-
-        turn = stack.enter_context(tc.psum_pool(name="turn", bufs=4))
-        sums = stack.enter_context(tc.psum_pool(name="sums", bufs=2))
-        total = stack.enter_context(tc.psum_pool(name="total", bufs=1))
-
-        pooled = total.tile([P, LAYERS * S], F32)
-
-        units = []
-        for t in range(N_TILES + LEAD):
-            if t < N_TILES:
-                units.append((0, t))
-            if t >= LEAD:
-                units.append((1, t - LEAD))
+        units = [(0, 0)]
+        for t in range(1, N_TILES):
+            units.extend([(0, t), (1, t - 1)])
+        units.append((1, N_TILES - 1))
         chunks = [(layer, t, c) for (layer, t) in units for c in range(CHUNKS)]
 
         z_rows, z_grouped, z_codes, z_scales, acc, o12 = {}, {}, {}, {}, {}, {}
@@ -147,13 +156,12 @@ def tile_cin_pa_kernel(tc, x, x1, w1, b1, w2, b2, out):
                 )
             else:
                 for i in range(I_CHUNK):
-                    nc.vector.tensor_scalar(
-                        out=z[:, FK * i : FK * (i + 1)],
-                        in0=o12[t][:, 0:S],
-                        scalar1=x_scalar[:, m, h, first_i + i : first_i + i + 1],
-                        scalar2=None,
-                        op0=MULT,
-                    )
+                    x_i = x_scalar[:, m, h, first_i + i : first_i + i + 1]
+                    z_i = z[:, FK * i : FK * (i + 1)]
+                    if i % SCALAR_EVERY == SCALAR_EVERY - 1:
+                        nc.scalar.activation(out=z_i, in_=o12[t][:, 0:S], func=COPY, scale=x_i)
+                    else:
+                        nc.vector.tensor_scalar(out=z_i, in0=o12[t][:, 0:S], scalar1=x_i, scalar2=None, op0=MULT)
 
         def turn_to_k(step):
             words = z_rows[step][:].bitcast(F32)
@@ -196,7 +204,7 @@ def tile_cin_pa_kernel(tc, x, x1, w1, b1, w2, b2, out):
             if c < CHUNKS - 1:
                 return
             if layer == 0:
-                o12[t] = stage.tile([P, LAYERS * S], F32, name="o12", bufs=LEAD + 2)
+                o12[t] = stage.tile([P, LAYERS * S], F32, name="o12")
             nc.vector.tensor_tensor(
                 out=o12[t][:, S * layer : S * (layer + 1)], in0=group[:], in1=bias_f[:, layer, :], op=ADD
             )
@@ -211,16 +219,21 @@ def tile_cin_pa_kernel(tc, x, x1, w1, b1, w2, b2, out):
                 )
 
         for step in range(len(chunks) + 3):
-            if 0 <= step - 3 < len(chunks):
-                multiply(step - 3)
-            if 0 <= step - 2 < len(chunks):
-                quantise(step - 2)
-            if 0 <= step - 1 < len(chunks):
-                turn_to_k(step - 1)
             if step < len(chunks):
                 form_products(step)
-            if 2 * step < PASSES:
-                prepare_weights(1, 2 * step, 2, nc.scalar.copy)
+            if step < CHUNKS:
+                prepare_weights(0, CHUNK * step, 2, nc.scalar.copy)
+                prepare_weights(0, CHUNK * step + 2, 2, nc.vector.tensor_copy)
+            elif step < 3 * CHUNKS:
+                prepare_weights(1, 2 * (step - CHUNKS), 2, nc.scalar.copy)
+            if step % (4 * CHUNKS) == 2 * CHUNKS and step // (4 * CHUNKS) < 3:
+                turn_x1(step // (4 * CHUNKS) + 1)
+            if 0 <= step - 1 < len(chunks):
+                turn_to_k(step - 1)
+            if 0 <= step - 2 < len(chunks):
+                quantise(step - 2)
+            if 0 <= step - 3 < len(chunks):
+                multiply(step - 3)
 
         result = keep.tile([P, LAYERS * S], F32)
         nc.vector.tensor_copy(out=result[:], in_=pooled[:])

@@ -25,7 +25,8 @@ CHUNKS = PASSES // CHUNK
 I_PASS = K_PASS // FK
 I_CHUNK = CHUNK * I_PASS
 LAYERS = 2
-SCALAR_EVERY = 4
+SCALAR_EVERY = 3
+LEAD = 2
 
 FLOPS = LAYERS * 2 * N * K * S
 
@@ -86,14 +87,17 @@ def tile_cin_pa_kernel(tc, x, x1, w1, b1, w2, b2, out):
             axis=mybir.AxisListType.X,
             op=ADD,
         )
-        bias_f = keep.tile([P, LAYERS, S], F32)
-        nc.vector.tensor_copy(out=bias_f[:], in_=bias_bf[:])
+        b1_rows = keep.tile([P, S], F32)
+        nc.vector.tensor_copy(out=b1_rows[:], in_=bias_bf[:, 0, :])
+        late_bias = keep.tile([P, LAYERS * S], F32)
+        nc.vector.memset(late_bias[:, 0:S], 0.0)
+        nc.vector.tensor_scalar(out=late_bias[:, S : 2 * S], in0=bias_bf[:, 1, :], scalar1=float(D), scalar2=None, op0=MULT)
 
         x_scalar = keep.tile([P, 4, 2, F0], F32)
         x_pairs = keep.tile([P, 4, 2, F0, 2], BF16)
         x1_rows = keep.tile([P, N_TILES, FK], BF16)
-        head = stack.enter_context(tc.psum_pool(name="head", bufs=1))
-        x_t = head.tile([P, 4, P], BF16, tag="turned")
+        turn = stack.enter_context(tc.psum_pool(name="turn", bufs=4))
+        x_t = turn.tile([P, 4, P], BF16, tag="bank")
         for m in range(4):
             nc.tensor.transpose(x_t[:, m, :], x_fields[:, P * m : P * (m + 1)], ident_bf[:])
         x_flat = x_t[:].rearrange("p m c -> p (m c)")
@@ -104,7 +108,7 @@ def tile_cin_pa_kernel(tc, x, x1, w1, b1, w2, b2, out):
         )
 
         def turn_x1(quarter):
-            x1_t = head.tile([P, 2, P], BF16, tag="turned")
+            x1_t = turn.tile([P, 2, P], BF16, tag="bank")
             for r in range(2):
                 t = 2 * quarter + r
                 nc.tensor.transpose(x1_t[:, r, :], x1_fields[:, P * t : P * (t + 1)], ident_bf[:])
@@ -112,8 +116,7 @@ def tile_cin_pa_kernel(tc, x, x1, w1, b1, w2, b2, out):
 
         turn_x1(0)
 
-        turn = stack.enter_context(tc.psum_pool(name="turn", bufs=4))
-        sums = stack.enter_context(tc.psum_pool(name="sums", bufs=2))
+        sums = stack.enter_context(tc.psum_pool(name="sums", bufs=3))
         total = stack.enter_context(tc.psum_pool(name="total", bufs=1))
 
         w_codes = [keep.tile([P, PASSES, S], U32, name="w_codes%d" % l, align_bytes=64) for l in range(LAYERS)]
@@ -132,11 +135,13 @@ def tile_cin_pa_kernel(tc, x, x1, w1, b1, w2, b2, out):
                 in_=w_grouped[:].rearrange("p g s t -> p (g s t)"),
             )
 
-        units = [(0, 0)]
-        for t in range(1, N_TILES):
-            units.extend([(0, t), (1, t - 1)])
-        units.append((1, N_TILES - 1))
-        chunks = [(layer, t, c) for (layer, t) in units for c in range(CHUNKS)]
+        chunks = []
+        for t in range(N_TILES + LEAD):
+            for c in range(CHUNKS):
+                if t < N_TILES:
+                    chunks.append((0, t, c))
+                if t >= LEAD:
+                    chunks.append((1, t - LEAD, c))
 
         z_rows, z_grouped, z_codes, z_scales, acc, o12 = {}, {}, {}, {}, {}, {}
 
@@ -169,7 +174,7 @@ def tile_cin_pa_kernel(tc, x, x1, w1, b1, w2, b2, out):
             z_grouped[step] = grouped
             grouped_words = grouped[:].bitcast(F32).rearrange("p (a n u) -> p a n u", a=CHUNK, u=2)
             for half in range(CHUNK // 2):
-                bank = turn.tile([P, 2, 2, P], F32, name="bank")
+                bank = turn.tile([P, 2, 2, P], F32, tag="bank")
                 for a in range(2):
                     for u in range(2):
                         first = P * (4 * half + 2 * a + u)
@@ -204,11 +209,10 @@ def tile_cin_pa_kernel(tc, x, x1, w1, b1, w2, b2, out):
             if c < CHUNKS - 1:
                 return
             if layer == 0:
-                o12[t] = stage.tile([P, LAYERS * S], F32, name="o12")
-            nc.vector.tensor_tensor(
-                out=o12[t][:, S * layer : S * (layer + 1)], in0=group[:], in1=bias_f[:, layer, :], op=ADD
-            )
-            if layer == 1:
+                o12[t] = stage.tile([P, LAYERS * S], F32, name="o12", bufs=LEAD + 2)
+                nc.vector.tensor_tensor(out=o12[t][:, 0:S], in0=group[:], in1=b1_rows[:], op=ADD)
+            else:
+                nc.scalar.copy(out=o12[t][:, S : 2 * S], in_=group[:])
                 window = pool_first - B_TILE * t
                 nc.tensor.matmul(
                     out=pooled[:],
@@ -226,7 +230,7 @@ def tile_cin_pa_kernel(tc, x, x1, w1, b1, w2, b2, out):
                 prepare_weights(0, CHUNK * step + 2, 2, nc.vector.tensor_copy)
             elif step < 3 * CHUNKS:
                 prepare_weights(1, 2 * (step - CHUNKS), 2, nc.scalar.copy)
-            if step % (4 * CHUNKS) == 2 * CHUNKS and step // (4 * CHUNKS) < 3:
+            if step % (4 * CHUNKS) == CHUNKS and step // (4 * CHUNKS) < 3:
                 turn_x1(step // (4 * CHUNKS) + 1)
             if 0 <= step - 1 < len(chunks):
                 turn_to_k(step - 1)
@@ -236,5 +240,5 @@ def tile_cin_pa_kernel(tc, x, x1, w1, b1, w2, b2, out):
                 multiply(step - 3)
 
         result = keep.tile([P, LAYERS * S], F32)
-        nc.vector.tensor_copy(out=result[:], in_=pooled[:])
+        nc.vector.tensor_tensor(out=result[:], in0=pooled[:], in1=late_bias[:], op=ADD)
         nc.sync.dma_start(out=out[:, :], in_=result[0:B, :])

@@ -25,15 +25,17 @@ CHUNKS = PASSES // CHUNK
 I_PASS = K_PASS // FK
 I_CHUNK = CHUNK * I_PASS
 LAYERS = 2
-SCALAR_EVERY = 3
-LEAD = 2
+QUADS = 4
+QUAD = P // QUADS
+LEAD = 6
+SCALAR_EVERY_BESIDE = 2
+SCALAR_EVERY_ALONE = 4
 
 FLOPS = LAYERS * 2 * N * K * S
 
 
 def tile_cin_pa_kernel(tc, x, x1, w1, b1, w2, b2, out):
     nc = tc.nc
-    weights = (w1, w2)
     with ExitStack() as stack:
         keep = stack.enter_context(tc.tile_pool(name="keep", bufs=1))
         stage = stack.enter_context(tc.tile_pool(name="stage", bufs=3))
@@ -55,14 +57,17 @@ def tile_cin_pa_kernel(tc, x, x1, w1, b1, w2, b2, out):
         w_rows = [keep.tile([P, PASSES, 4, S], BF16, name="w_rows%d" % l) for l in range(LAYERS)]
 
         def load_weights(layer):
-            source = weights[layer].rearrange("(c u p e) s -> p c u (e s)", c=CHUNKS, p=P, e=2)
+            if layer == 0:
+                source = w1.rearrange("(c g p t) s -> p c g (t s)", c=CHUNKS, p=P, t=4)
+            else:
+                source = w2.rearrange("(c u p e) s -> p c u (e s)", c=CHUNKS, p=P, e=2)
             for c in range(CHUNKS):
-                nc.sync.dma_start(
-                    out=w_rows[layer][:, CHUNK * c : CHUNK * (c + 1), :, :].rearrange(
-                        "p g (u e) s -> p (g u) (e s)", e=2
-                    ),
-                    in_=source[:, c, :, :],
-                )
+                rows = w_rows[layer][:, CHUNK * c : CHUNK * (c + 1), :, :]
+                if layer == 0:
+                    rows = rows.rearrange("p g t s -> p g (t s)")
+                else:
+                    rows = rows.rearrange("p g (u e) s -> p (g u) (e s)", e=2)
+                nc.sync.dma_start(out=rows, in_=source[:, c, :, :])
 
         load_x1(0)
         bias_bf = keep.tile([P, LAYERS, S], BF16)
@@ -95,7 +100,8 @@ def tile_cin_pa_kernel(tc, x, x1, w1, b1, w2, b2, out):
 
         x_scalar = keep.tile([P, 4, 2, F0], F32)
         x_pairs = keep.tile([P, 4, 2, F0, 2], BF16)
-        x1_rows = keep.tile([P, N_TILES, FK], BF16)
+        x1_spread = keep.tile([P, N_TILES * P * 4], BF16)
+        x1_spread_words = x1_spread[:].bitcast(F32).rearrange("p (a n h) -> p a n h", a=N_TILES, h=2)
         turn = stack.enter_context(tc.psum_pool(name="turn", bufs=4))
         x_t = turn.tile([P, 4, P], BF16, tag="bank")
         for m in range(4):
@@ -109,10 +115,26 @@ def tile_cin_pa_kernel(tc, x, x1, w1, b1, w2, b2, out):
 
         def turn_x1(quarter):
             x1_t = turn.tile([P, 2, P], BF16, tag="bank")
-            for r in range(2):
-                t = 2 * quarter + r
-                nc.tensor.transpose(x1_t[:, r, :], x1_fields[:, P * t : P * (t + 1)], ident_bf[:])
-            nc.scalar.copy(out=x1_rows[:, 2 * quarter : 2 * quarter + 2, :], in_=x1_t[:])
+            x1_copies = stage.tile([P, 2, 2, QUADS, QUAD], F32)
+            for a in range(2):
+                t = 2 * quarter + a
+                nc.tensor.transpose(x1_t[:, a, :], x1_fields[:, P * t : P * (t + 1)], ident_bf[:])
+            for a in range(2):
+                nc.scalar.copy(
+                    out=x1_copies[:, a, :, :, :],
+                    in_=x1_t[:, a, :].bitcast(F32).rearrange("p (r h) -> p h r", h=2).unsqueeze(2)
+                    .to_broadcast([P, 2, QUADS, QUAD]),
+                )
+            bank = turn.tile([P, 2, 2, P], F32, tag="bank")
+            for a in range(2):
+                for h in range(2):
+                    nc.tensor.transpose(
+                        bank[:, a, h, :], x1_copies[:, a, h, :, :].rearrange("p q r -> p (q r)"), ident_f[:]
+                    )
+            nc.scalar.copy(
+                out=x1_spread_words[:, 2 * quarter : 2 * quarter + 2, :, :],
+                in_=bank[:].rearrange("p a h n -> p a n h"),
+            )
 
         turn_x1(0)
 
@@ -135,43 +157,60 @@ def tile_cin_pa_kernel(tc, x, x1, w1, b1, w2, b2, out):
                 in_=w_grouped[:].rearrange("p g s t -> p (g s t)"),
             )
 
+        per_layer = [[(layer, t, c) for t in range(N_TILES) for c in range(CHUNKS)] for layer in range(LAYERS)]
         chunks = []
-        for t in range(N_TILES + LEAD):
-            for c in range(CHUNKS):
-                if t < N_TILES:
-                    chunks.append((0, t, c))
-                if t >= LEAD:
-                    chunks.append((1, t - LEAD, c))
+        for k in range(N_TILES * CHUNKS + LEAD):
+            if k < N_TILES * CHUNKS:
+                chunks.append(per_layer[0][k])
+            if k >= LEAD:
+                chunks.append(per_layer[1][k - LEAD])
+        last_of_layer_1 = chunks.index(per_layer[0][-1])
 
-        z_rows, z_grouped, z_codes, z_scales, acc, o12 = {}, {}, {}, {}, {}, {}
+        rows_n, z_grouped, z_codes, z_scales, acc, o12 = {}, {}, {}, {}, {}, {}
 
-        def form_products(step):
+        def start_chunk(step):
             layer, t, c = chunks[step]
             m, h = t % 4, t // 4
             first_i = I_CHUNK * c
-            z = stage.tile([P, I_CHUNK * FK], BF16, name="z_rows")
-            z_rows[step] = z
             if layer == 0:
-                shape = [P, I_CHUNK, FK // 2, 2]
-                nc.vector.tensor_tensor(
-                    out=z[:].rearrange("p (i j r) -> p i j r", i=I_CHUNK, r=2),
-                    in0=x1_rows[:, t, :].rearrange("p (j r) -> p j r", r=2).unsqueeze(1).to_broadcast(shape),
-                    in1=x_pairs[:, m, h, first_i : first_i + I_CHUNK, :].unsqueeze(2).to_broadcast(shape),
-                    op=MULT,
+                x_copies = stage.tile([P, CHUNK, QUADS, QUAD], F32)
+                rows_n[step] = x_copies
+                words = x_pairs[:, m, h, first_i : first_i + I_CHUNK, :].rearrange("p i r -> p (i r)").bitcast(F32)
+                nc.scalar.copy(
+                    out=x_copies[:],
+                    in_=words.rearrange("p (a q) -> p a q", q=QUADS).unsqueeze(3).to_broadcast([P, CHUNK, QUADS, QUAD]),
                 )
-            else:
-                for i in range(I_CHUNK):
-                    x_i = x_scalar[:, m, h, first_i + i : first_i + i + 1]
-                    z_i = z[:, FK * i : FK * (i + 1)]
-                    if i % SCALAR_EVERY == SCALAR_EVERY - 1:
-                        nc.scalar.activation(out=z_i, in_=o12[t][:, 0:S], func=COPY, scale=x_i)
-                    else:
-                        nc.vector.tensor_scalar(out=z_i, in0=o12[t][:, 0:S], scalar1=x_i, scalar2=None, op0=MULT)
+                return
+            z = stage.tile([P, I_CHUNK * FK], BF16, name="z_rows")
+            rows_n[step] = z
+            every = SCALAR_EVERY_BESIDE if step < last_of_layer_1 else SCALAR_EVERY_ALONE
+            for i in range(I_CHUNK):
+                x_i = x_scalar[:, m, h, first_i + i : first_i + i + 1]
+                z_i = z[:, FK * i : FK * (i + 1)]
+                if i % every == every - 1:
+                    nc.scalar.activation(out=z_i, in_=o12[t][:, 0:S], func=COPY, scale=x_i)
+                else:
+                    nc.vector.tensor_scalar(out=z_i, in0=o12[t][:, 0:S], scalar1=x_i, scalar2=None, op0=MULT)
 
         def turn_to_k(step):
-            words = z_rows[step][:].bitcast(F32)
+            layer, t, c = chunks[step]
             grouped = stage.tile([P, CHUNK * P * 4], BF16, name="z_grouped", align_bytes=64)
             z_grouped[step] = grouped
+            if layer == 0:
+                bank = turn.tile([P, CHUNK, P], F32, tag="bank")
+                for a in range(CHUNK):
+                    nc.tensor.transpose(bank[:, a, :], rows_n[step][:, a, :, :].rearrange("p q r -> p (q r)"), ident_f[:])
+                shape = [P, CHUNK, P, 2, 2]
+                nc.vector.tensor_tensor(
+                    out=grouped[:].rearrange("p (a n h l) -> p a n h l", a=CHUNK, h=2, l=2),
+                    in0=x1_spread[:, 4 * P * t : 4 * P * (t + 1)]
+                    .rearrange("p (n h l) -> p n h l", h=2, l=2).unsqueeze(1).to_broadcast(shape),
+                    in1=bank[:].rearrange("p a n -> p (a n)").bitcast(BF16)
+                    .rearrange("p (a n l) -> p a n l", a=CHUNK, l=2).unsqueeze(3).to_broadcast(shape),
+                    op=MULT,
+                )
+                return
+            words = rows_n[step][:].bitcast(F32)
             grouped_words = grouped[:].bitcast(F32).rearrange("p (a n u) -> p a n u", a=CHUNK, u=2)
             for half in range(CHUNK // 2):
                 bank = turn.tile([P, 2, 2, P], F32, tag="bank")
@@ -209,7 +248,7 @@ def tile_cin_pa_kernel(tc, x, x1, w1, b1, w2, b2, out):
             if c < CHUNKS - 1:
                 return
             if layer == 0:
-                o12[t] = stage.tile([P, LAYERS * S], F32, name="o12", bufs=LEAD + 2)
+                o12[t] = stage.tile([P, LAYERS * S], F32, name="o12", bufs=4)
                 nc.vector.tensor_tensor(out=o12[t][:, 0:S], in0=group[:], in1=b1_rows[:], op=ADD)
             else:
                 nc.scalar.copy(out=o12[t][:, S : 2 * S], in_=group[:])
@@ -224,13 +263,13 @@ def tile_cin_pa_kernel(tc, x, x1, w1, b1, w2, b2, out):
 
         for step in range(len(chunks) + 3):
             if step < len(chunks):
-                form_products(step)
+                start_chunk(step)
             if step < CHUNKS:
                 prepare_weights(0, CHUNK * step, 2, nc.scalar.copy)
                 prepare_weights(0, CHUNK * step + 2, 2, nc.vector.tensor_copy)
             elif step < 3 * CHUNKS:
                 prepare_weights(1, 2 * (step - CHUNKS), 2, nc.scalar.copy)
-            if step % (4 * CHUNKS) == CHUNKS and step // (4 * CHUNKS) < 3:
+            if step % (4 * CHUNKS) == LEAD and step // (4 * CHUNKS) < 3:
                 turn_x1(step // (4 * CHUNKS) + 1)
             if 0 <= step - 1 < len(chunks):
                 turn_to_k(step - 1)

from contextlib import ExitStack

import concourse.mybir as mybir
from concourse.masks import make_identity

F32 = mybir.dt.float32
BF16 = mybir.dt.bfloat16
U32 = mybir.dt.uint32
U8 = mybir.dt.uint8
FP8X4 = mybir.dt.float8_e4m3fn_x4
MULT = mybir.AluOpType.mult
ADD = mybir.AluOpType.add
COPY = mybir.ActivationFunctionType.Copy

P = 128
B, F0, FK, S, D = 64, 64, 128, 128, 16
N = B * D
K = F0 * FK
K_PASS = 4 * P
PASSES = K // K_PASS
N_TILES = N // P
B_TILE = P // D
CHUNK = 4
CHUNKS = PASSES // CHUNK
I_PASS = K_PASS // FK
I_CHUNK = CHUNK * I_PASS
LAYERS = 2
QUADS = 4
QUAD = P // QUADS
LEAD = 6
SCALAR_EVERY_BESIDE = 2
SCALAR_EVERY_ALONE = 4

FLOPS = LAYERS * 2 * N * K * S


def tile_cin_pa_kernel(tc, x, x1, w1, b1, w2, b2, out):
    nc = tc.nc
    with ExitStack() as stack:
        keep = stack.enter_context(tc.tile_pool(name="keep", bufs=1))
        stage = stack.enter_context(tc.tile_pool(name="stage", bufs=3))

        x_fields = keep.tile([P, N // 2], BF16)
        for h in range(2):
            nc.sync.dma_start(
                out=x_fields[F0 * h : F0 * (h + 1), :].rearrange("i (b d) -> i b d", d=D),
                in_=x[B // 2 * h : B // 2 * (h + 1)].rearrange("b i d -> i b d"),
            )
        x1_fields = keep.tile([P, N], BF16)

        def load_x1(quarter):
            nc.sync.dma_start(
                out=x1_fields[:, N // 4 * quarter : N // 4 * (quarter + 1)].rearrange("j (b d) -> j b d", d=D),
                in_=x1[B // 4 * quarter : B // 4 * (quarter + 1)].rearrange("b j d -> j b d"),
            )

        w_rows = [keep.tile([P, PASSES, 4, S], BF16, name="w_rows%d" % l) for l in range(LAYERS)]

        def load_weights(layer):
            if layer == 0:
                source = w1.rearrange("(c g p t) s -> p c g (t s)", c=CHUNKS, p=P, t=4)
            else:
                source = w2.rearrange("(c u p e) s -> p c u (e s)", c=CHUNKS, p=P, e=2)
            for c in range(CHUNKS):
                rows = w_rows[layer][:, CHUNK * c : CHUNK * (c + 1), :, :]
                if layer == 0:
                    rows = rows.rearrange("p g t s -> p g (t s)")
                else:
                    rows = rows.rearrange("p g (u e) s -> p (g u) (e s)", e=2)
                nc.sync.dma_start(out=rows, in_=source[:, c, :, :])

        load_x1(0)
        bias_bf = keep.tile([P, LAYERS, S], BF16)
        nc.sync.dma_start(out=bias_bf[:, 0, :], in_=b1.partition_broadcast(P))
        nc.sync.dma_start(out=bias_bf[:, 1, :], in_=b2.partition_broadcast(P))
        load_weights(0)
        load_x1(1)
        load_weights(1)
        load_x1(2)
        load_x1(3)

        ident_bf = keep.tile([P, P], BF16)
        make_identity(nc, ident_bf[:])
        ident_f = keep.tile([P, P], F32)
        make_identity(nc, ident_f[:])
        pool_first = B - B_TILE
        pool_sel = keep.tile([P, pool_first + P], F32)
        nc.vector.memset(pool_sel[:], 0.0)
        nc.vector.tensor_reduce(
            out=pool_sel[:, pool_first : pool_first + B_TILE],
            in_=ident_f[:].rearrange("p (b d) -> p b d", d=D),
            axis=mybir.AxisListType.X,
            op=ADD,
        )
        b1_rows = keep.tile([P, S], F32)
        nc.vector.tensor_copy(out=b1_rows[:], in_=bias_bf[:, 0, :])
        late_bias = keep.tile([P, LAYERS * S], F32)
        nc.vector.memset(late_bias[:, 0:S], 0.0)
        nc.vector.tensor_scalar(out=late_bias[:, S : 2 * S], in0=bias_bf[:, 1, :], scalar1=float(D), scalar2=None, op0=MULT)

        x_scalar = keep.tile([P, 4, 2, F0], F32)
        x_pairs = keep.tile([P, 4, 2, F0, 2], BF16)
        x1_spread = keep.tile([P, N_TILES * P * 4], BF16)
        x1_spread_words = x1_spread[:].bitcast(F32).rearrange("p (a n h) -> p a n h", a=N_TILES, h=2)
        turn = stack.enter_context(tc.psum_pool(name="turn", bufs=4))
        x_t = turn.tile([P, 4, P], BF16, tag="bank")
        for m in range(4):
            nc.tensor.transpose(x_t[:, m, :], x_fields[:, P * m : P * (m + 1)], ident_bf[:])
        x_flat = x_t[:].rearrange("p m c -> p (m c)")
        nc.vector.tensor_copy(out=x_scalar[:].rearrange("p m h i -> p (m h i)"), in_=x_flat)
        nc.scalar.copy(
            out=x_pairs[:].rearrange("p m h i r -> p (m h i) r"),
            in_=x_flat.unsqueeze(2).to_broadcast([P, 4 * P, 2]),
        )

        def turn_x1(quarter):
            x1_t = turn.tile([P, 2, P], BF16, tag="bank")
            x1_copies = stage.tile([P, 2, 2, QUADS, QUAD], F32)
            for a in range(2):
                t = 2 * quarter + a
                nc.tensor.transpose(x1_t[:, a, :], x1_fields[:, P * t : P * (t + 1)], ident_bf[:])
            for a in range(2):
                nc.scalar.copy(
                    out=x1_copies[:, a, :, :, :],
                    in_=x1_t[:, a, :].bitcast(F32).rearrange("p (r h) -> p h r", h=2).unsqueeze(2)
                    .to_broadcast([P, 2, QUADS, QUAD]),
                )
            bank = turn.tile([P, 2, 2, P], F32, tag="bank")
            for a in range(2):
                for h in range(2):
                    nc.tensor.transpose(
                        bank[:, a, h, :], x1_copies[:, a, h, :, :].rearrange("p q r -> p (q r)"), ident_f[:]
                    )
            nc.scalar.copy(
                out=x1_spread_words[:, 2 * quarter : 2 * quarter + 2, :, :],
                in_=bank[:].rearrange("p a h n -> p a n h"),
            )

        turn_x1(0)

        sums = stack.enter_context(tc.psum_pool(name="sums", bufs=3))
        total = stack.enter_context(tc.psum_pool(name="total", bufs=1))

        w_codes = [keep.tile([P, PASSES, S], U32, name="w_codes%d" % l, align_bytes=64) for l in range(LAYERS)]
        w_scales = [keep.tile([P, PASSES, S], U8, name="w_scales%d" % l, align_bytes=64) for l in range(LAYERS)]
        pooled = total.tile([P, LAYERS * S], F32)

        def prepare_weights(layer, first, count, copy):
            w_grouped = stage.tile([P, count, S, 4], BF16, align_bytes=64, tag="w_grouped%d" % count)
            copy(
                out=w_grouped[:],
                in_=w_rows[layer][:, first : first + count, :, :].rearrange("p g t s -> p g s t"),
            )
            nc.vector.quantize_mx(
                out=w_codes[layer][:, first : first + count, :].rearrange("p g s -> p (g s)").bitcast(FP8X4),
                scales=w_scales[layer][:, first : first + count, :].rearrange("p g s -> p (g s)"),
                in_=w_grouped[:].rearrange("p g s t -> p (g s t)"),
            )

        per_layer = [[(layer, t, c) for t in range(N_TILES) for c in range(CHUNKS)] for layer in range(LAYERS)]
        chunks = []
        for k in range(N_TILES * CHUNKS + LEAD):
            if k < N_TILES * CHUNKS:
                chunks.append(per_layer[0][k])
            if k >= LEAD:
                chunks.append(per_layer[1][k - LEAD])
        last_of_layer_1 = chunks.index(per_layer[0][-1])

        rows_n, z_grouped, z_codes, z_scales, acc, o12 = {}, {}, {}, {}, {}, {}

        def start_chunk(step):
            layer, t, c = chunks[step]
            m, h = t % 4, t // 4
            first_i = I_CHUNK * c
            if layer == 0:
                x_copies = stage.tile([P, CHUNK, QUADS, QUAD], F32)
                rows_n[step] = x_copies
                words = x_pairs[:, m, h, first_i : first_i + I_CHUNK, :].rearrange("p i r -> p (i r)").bitcast(F32)
                nc.scalar.copy(
                    out=x_copies[:],
                    in_=words.rearrange("p (a q) -> p a q", q=QUADS).unsqueeze(3).to_broadcast([P, CHUNK, QUADS, QUAD]),
                )
                return
            z = stage.tile([P, I_CHUNK * FK], BF16, name="z_rows")
            rows_n[step] = z
            every = SCALAR_EVERY_BESIDE if step < last_of_layer_1 else SCALAR_EVERY_ALONE
            for i in range(I_CHUNK):
                x_i = x_scalar[:, m, h, first_i + i : first_i + i + 1]
                z_i = z[:, FK * i : FK * (i + 1)]
                if i % every == every - 1:
                    nc.scalar.activation(out=z_i, in_=o12[t][:, 0:S], func=COPY, scale=x_i)
                else:
                    nc.vector.tensor_scalar(out=z_i, in0=o12[t][:, 0:S], scalar1=x_i, scalar2=None, op0=MULT)

        def turn_to_k(step):
            layer, t, c = chunks[step]
            grouped = stage.tile([P, CHUNK * P * 4], BF16, name="z_grouped", align_bytes=64)
            z_grouped[step] = grouped
            if layer == 0:
                bank = turn.tile([P, CHUNK, P], F32, tag="bank")
                for a in range(CHUNK):
                    nc.tensor.transpose(bank[:, a, :], rows_n[step][:, a, :, :].rearrange("p q r -> p (q r)"), ident_f[:])
                shape = [P, CHUNK, P, 2, 2]
                nc.vector.tensor_tensor(
                    out=grouped[:].rearrange("p (a n h l) -> p a n h l", a=CHUNK, h=2, l=2),
                    in0=x1_spread[:, 4 * P * t : 4 * P * (t + 1)]
                    .rearrange("p (n h l) -> p n h l", h=2, l=2).unsqueeze(1).to_broadcast(shape),
                    in1=bank[:].rearrange("p a n -> p (a n)").bitcast(BF16)
                    .rearrange("p (a n l) -> p a n l", a=CHUNK, l=2).unsqueeze(3).to_broadcast(shape),
                    op=MULT,
                )
                return
            words = rows_n[step][:].bitcast(F32)
            grouped_words = grouped[:].bitcast(F32).rearrange("p (a n u) -> p a n u", a=CHUNK, u=2)
            for half in range(CHUNK // 2):
                bank = turn.tile([P, 2, 2, P], F32, tag="bank")
                for a in range(2):
                    for u in range(2):
                        first = P * (4 * half + 2 * a + u)
                        nc.tensor.transpose(bank[:, a, u, :], words[:, first : first + P], ident_f[:])
                nc.scalar.copy(
                    out=grouped_words[:, 2 * half : 2 * half + 2, :, :],
                    in_=bank[:].rearrange("p a u n -> p a n u"),
                )

        def quantise(step):
            codes = stage.tile([P, CHUNK * P], U32, name="z_codes", align_bytes=64)
            scales = stage.tile([P, CHUNK * P], U8, name="z_scales", align_bytes=64)
            z_codes[step], z_scales[step] = codes, scales
            nc.vector.quantize_mx(out=codes[:].bitcast(FP8X4), scales=scales[:], in_=z_grouped[step][:])

        def multiply(step):
            layer, t, c = chunks[step]
            if c == 0:
                acc[(layer, t)] = sums.tile([P, S], F32, name="acc")
            group = acc[(layer, t)]
            for a in range(CHUNK):
                g = CHUNK * c + a
                nc.tensor.matmul_mx(
                    out=group[:],
                    lhsT=z_codes[step][:, P * a : P * (a + 1)].bitcast(FP8X4),
                    lhsT_scale=z_scales[step][:, P * a : P * (a + 1)],
                    rhs=w_codes[layer][:, g, :].bitcast(FP8X4),
                    rhs_scale=w_scales[layer][:, g, :],
                    start=(g == 0),
                    stop=(g == PASSES - 1),
                )
            if c < CHUNKS - 1:
                return
            if layer == 0:
                o12[t] = stage.tile([P, LAYERS * S], F32, name="o12", bufs=4)
                nc.vector.tensor_tensor(out=o12[t][:, 0:S], in0=group[:], in1=b1_rows[:], op=ADD)
            else:
                nc.scalar.copy(out=o12[t][:, S : 2 * S], in_=group[:])
                window = pool_first - B_TILE * t
                nc.tensor.matmul(
                    out=pooled[:],
                    lhsT=pool_sel[:, window : window + P],
                    rhs=o12[t][:],
                    start=(t == 0),
                    stop=(t == N_TILES - 1),
                )

        for step in range(len(chunks) + 3):
            if step < len(chunks):
                start_chunk(step)
            if step < CHUNKS:
                prepare_weights(0, CHUNK * step, 2, nc.scalar.copy)
                prepare_weights(0, CHUNK * step + 2, 2, nc.vector.tensor_copy)
            elif step < 3 * CHUNKS:
                prepare_weights(1, 2 * (step - CHUNKS), 2, nc.scalar.copy)
            if step % (4 * CHUNKS) == LEAD and step // (4 * CHUNKS) < 3:
                turn_x1(step // (4 * CHUNKS) + 1)
            if 0 <= step - 1 < len(chunks):
                turn_to_k(step - 1)
            if 0 <= step - 2 < len(chunks):
                quantise(step - 2)
            if 0 <= step - 3 < len(chunks):
                multiply(step - 3)

        result = keep.tile([P, LAYERS * S], F32)
        nc.vector.tensor_tensor(out=result[:], in0=pooled[:], in1=late_bias[:], op=ADD)
        nc.sync.dma_start(out=out[:, :], in_=result[0:B, :])
